import numpy as np
import ml_dtypes


def mxq(x, axis, fmt="e4m3"):
    dtype, down = {"e4m3": (ml_dtypes.float8_e4m3fn, 7), "e5m2": (ml_dtypes.float8_e5m2, 14)}[fmt]
    v = np.moveaxis(np.asarray(x, np.float32).astype(ml_dtypes.bfloat16).astype(np.float64), axis, -1)
    blocks = v.reshape(v.shape[:-1] + (-1, 32))
    amax = np.abs(blocks).max(-1, keepdims=True)
    byte = np.maximum(np.where(amax > 0, np.frexp(amax)[1] - 1 + 127, 0) - down, 1)
    scale = np.exp2(byte - 127.0)
    codes = (blocks / scale).astype(np.float32).astype(dtype).astype(np.float64)
    return np.moveaxis((codes * scale).reshape(v.shape), -1, axis)


WIDE = False


def mx_kscale(k):
    if not WIDE:
        return np.ones(k)
    levels = np.array([10, -10, 5, -5, 0])
    if k % 512:
        return np.exp2(np.random.permutation(np.resize(levels, k // 32))).repeat(32)
    a = np.empty((k // 512, 16))
    for p in range(k // 512):
        a[p, :8] = np.random.permutation(np.resize(levels, 8))
        for g in range(8):
            far = levels[np.abs(levels - a[p, g]) >= 10]
            a[p, g + 8] = far[np.random.randint(len(far))]
    return np.exp2(a.ravel()).repeat(32)


BF16 = ml_dtypes.bfloat16


def bf(x):
    return np.asarray(x, np.float32).astype(BF16)


def f64(x):
    return np.asarray(x).astype(np.float64)


B, K, G, D, FF, F, P, H = 16, 64, 128, 1024, 2048, 2048, 7, 8
NC = K * G
EPS = 1e-5


def layernorm(x, g, b):
    m = x.mean(-1, keepdims=True)
    v = ((x - m) ** 2).mean(-1, keepdims=True)
    return (x - m) / np.sqrt(v + EPS) * g + b


def setup_inputs():
    n = np.random.standard_normal
    s, t = mx_kscale(FF), mx_kscale(D)
    return {
        "ff_hid": bf(np.maximum(n((B, K, FF)), 0.0) * s),
        "tgt": bf(n((B, K, D))),
        "w2": bf(n((FF, D)) / np.sqrt(FF) / s[:, None]),
        "b2": bf(0.1 * n(D)),
        "g3": bf((1.0 + 0.1 * n(D)) * t),
        "be3": bf(0.1 * n(D) * t),
        "dup_pool": bf(n((K, D, G)) / np.sqrt(D) / t[None, :, None]),
        "dup_bias": bf(0.2 * n(NC)),
    }


def reference(ff_hid, tgt, w2, b2, g3, be3, dup_pool, dup_bias):
    ff = (mxq(f64(ff_hid), 2, "e4m3") @ mxq(f64(w2), 0, "e4m3")) + f64(b2)
    h = layernorm(f64(tgt) + ff, f64(g3), f64(be3))
    out_extrap = (mxq(h, 2, "e4m3").transpose(1, 0, 2) @ mxq(f64(dup_pool), 1, "e4m3")).transpose(1, 0, 2)
    return out_extrap.reshape(B, -1)[:, :NC] + f64(dup_bias)

@@ -1,0 +1,408 @@
+from contextlib import ExitStack
+
+import concourse.mybir as mybir
+from concourse.masks import make_identity
+
+F32 = mybir.dt.float32
+BF16 = mybir.dt.bfloat16
+U32 = mybir.dt.uint32
+U8 = mybir.dt.uint8
+I32 = mybir.dt.int32
+FP8X4 = mybir.dt.float8_e4m3fn_x4
+ALU = mybir.AluOpType
+ACT = mybir.ActivationFunctionType
+
+P = 128
+NB = 16
+NK = 64
+NG = 128
+D = 1024
+FF = 2048
+NT = 8
+EPS = 1e-5
+FLOPS = 2 * NB * NK * FF * D + 2 * NB * NK * D * NG
+
+V_BLOCKS = 4
+S_FIRST = 1
+LAG = {"FT": 0, "FE": 2, "FQ": 3, "T": 3, "MM": 5, "E": 7, "SQ": 8, "R": 8, "ZE": 11, "HR": 11, "HQ": 12, "O2": 14, "OE": 3, "OC": 7}
+SPARSE_UNTIL = 18
+PRE_BULK = 4
+PRE_F = 2
+PRE_T = 4
+GAIN_LOAD_AFTER = 6
+CONST_TICK = 9
+
+
+def bulk_plan():
+    plan = [("w", g) for g in range(4)]
+    s = 0
+    while s < 16:
+        m = len(plan)
+        if m < SPARSE_UNTIL and m % 2 == 0:
+            plan.append(None)
+        else:
+            plan.append(("x", s))
+            s += 1
+    return plan
+
+
+def tile_at(m, lag):
+    t = m - lag
+    if t >= 0 and t % 2 == 0 and t // 2 < NT:
+        return t // 2
+    return -1
+
+
+def tile_mldecoder_pb_kernel(tc, ff_hid, tgt, w2, b2, g3, be3, dup_pool, dup_bias, out):
+    nc = tc.nc
+    ffv = ff_hid.rearrange("b (kk i) f -> (b kk) i f", i=8)
+    tgv = tgt.rearrange("b (kk i) d -> (b kk) i d", i=8)
+    w2v = w2.rearrange("(g p j) n -> g p (j n)", g=4, j=4)
+    dv = dup_pool.rearrange("(kk i) (c p j) g -> i c p kk (j g)", i=8, c=2, j=4)
+    outv = out.rearrange("b (kk x) -> (b kk) x", kk=8)
+    plan = bulk_plan()
+    q_tick = {}
+    for m in range(len(plan)):
+        if plan[m] is not None:
+            q_tick[plan[m]] = m + 1
+    o_tick = [max(2 * i + LAG["O2"], q_tick[("x", 2 * i + 1)] + 1) for i in range(NT)]
+    n_ticks = max(o_tick) + LAG["OC"] + 1
+
+    with ExitStack() as ctx:
+        const = ctx.enter_context(tc.tile_pool(name="const", bufs=1))
+        keep = ctx.enter_context(tc.tile_pool(name="keep", bufs=1))
+        rawp = ctx.enter_context(tc.tile_pool(name="rawp", bufs=6))
+        frawp = ctx.enter_context(tc.tile_pool(name="frawp", bufs=3))
+        grpp = ctx.enter_context(tc.tile_pool(name="grpp", bufs=3))
+        xp = ctx.enter_context(tc.tile_pool(name="xp", bufs=5))
+        work1 = ctx.enter_context(tc.tile_pool(name="work1", bufs=1))
+        work2 = ctx.enter_context(tc.tile_pool(name="work2", bufs=2))
+        work4 = ctx.enter_context(tc.tile_pool(name="work4", bufs=4))
+        small = ctx.enter_context(tc.tile_pool(name="small", bufs=4))
+        psum = ctx.enter_context(tc.psum_pool(name="psum", bufs=2))
+
+        brow = grpp.tile([P, 4096], BF16, tag="grp", align_bytes=64)
+        nc.vector.memset(brow[:, 0:D].bitcast(I32), 0)
+        nc.sync.dma_start(out=brow[0:1, 0:D], in_=b2.rearrange("(o d) -> o d", o=1))
+        g3r = const.tile([P, 2, 4], BF16)
+        be3r = const.tile([P, 2, 4], BF16)
+        braw = const.tile([P, P], BF16)
+        nc.vector.memset(braw[:].bitcast(I32), 0)
+        nc.sync.dma_start(out=braw[0:NK, :], in_=dup_bias.rearrange("(k g) -> k g", g=NG))
+
+        wanted = []
+        for m in range(len(plan)):
+            if plan[m] is not None:
+                wanted.append((m - PRE_BULK, plan[m]))
+        for t in range(NT):
+            wanted.append((2 * t + LAG["FT"] - PRE_F, ("f", t)))
+            if t % 2 == 0:
+                wanted.append((2 * t + LAG["T"] - PRE_T, ("t", t // 2)))
+        raws = {}
+        for item in sorted(wanted, key=lambda pair: pair[0]):
+            if len(raws) == GAIN_LOAD_AFTER:
+                nc.sync.dma_start(out=g3r[:], in_=g3.rearrange("(c p t) -> p c t", c=2, t=4))
+                nc.sync.dma_start(out=be3r[:], in_=be3.rearrange("(c p t) -> p c t", c=2, t=4))
+            kind = item[1][0]
+            idx = item[1][1]
+            if kind == "w":
+                wraw = rawp.tile([P, 4, D], BF16, tag="raw")
+                nc.sync.dma_start(out=wraw[:].rearrange("p j n -> p (j n)"), in_=w2v[idx])
+                raws[item[1]] = wraw[:].rearrange("p t (k n) -> p k t n", k=8)
+            elif kind == "x":
+                xraw = rawp.tile([P, 8, 512], BF16, tag="raw")
+                nc.sync.dma_start(out=xraw[:], in_=dv[idx // 2, idx % 2])
+                raws[item[1]] = xraw[:].rearrange("p k (t n) -> p k t n", t=4)
+            elif kind == "f":
+                fraw = frawp.tile([P, FF], BF16, tag="fraw")
+                nc.sync.dma_start(out=fraw[:], in_=ffv[:, idx, :])
+                raws[item[1]] = fraw
+            else:
+                traw = work2.tile([P, 2, D], BF16, tag="traw")
+                nc.sync.dma_start(out=traw[:], in_=tgv[:, 2 * idx:2 * idx + 2, :])
+                raws[item[1]] = traw
+
+        eps = const.tile([P, 1], F32)
+        nc.vector.memset(eps[:], EPS)
+        warm = const.tile([P, 1], F32)
+        nc.scalar.activation(out=warm[:], in_=eps[:], func=ACT.Sqrt)
+        ident = const.tile([P, P], F32)
+        make_identity(nc, ident[:])
+        identb = const.tile([P, P], BF16)
+        make_identity(nc, identb[:])
+        perm = const.tile([P, P], F32)
+        nc.vector.tensor_copy(
+            out=perm[:].rearrange("p (k b) -> p k b", k=8),
+            in_=ident[:].rearrange("p (b k) -> p k b", k=8),
+        )
+        ones = const.tile([P, P], BF16)
+        nc.vector.memset(ones[:], 1.0)
+        b2bc = const.tile([P, D], BF16)
+        g3T = const.tile([P, 8], F32)
+        be3T = const.tile([P, 8], F32)
+        bexp = const.tile([P, NT, P], F32)
+        o_all = const.tile([P, D], F32)
+
+        w2c = keep.tile([P, 4, D], U32, align_bytes=64)
+        w2s = keep.tile([P, 4, D], U8, align_bytes=64)
+        fc = keep.tile([P, NT, 512], U32, align_bytes=64)
+        fs = keep.tile([P, NT, 512], U8, align_bytes=64)
+        hc = keep.tile([P, NT, 256], U32, align_bytes=64)
+        hs = keep.tile([P, NT, 256], U8, align_bytes=64)
+
+        live = {}
+
+        def b2_spread():
+            for h in range(2):
+                bb = psum.tile([P, 512], F32, tag="mm")
+                nc.tensor.matmul(out=bb[:], lhsT=ones[:], rhs=brow[:, 512 * h:512 * h + 512], start=True, stop=True)
+                nc.scalar.copy(out=b2bc[:, 512 * h:512 * h + 512], in_=bb[:])
+
+        def consts():
+            nc.vector.tensor_copy(out=g3T[:], in_=g3r[:].rearrange("p c t -> p (c t)"))
+            nc.vector.tensor_copy(out=be3T[:], in_=be3r[:].rearrange("p c t -> p (c t)"))
+            bps = psum.tile([P, P], BF16, tag="s2")
+            nc.tensor.transpose(bps[:], braw[:], identb[:])
+            nc.scalar.copy(
+                out=bexp[:].rearrange("p i (b k) -> p i b k", k=8),
+                in_=bps[:, 0:NK].rearrange("p (k i) -> p i k", i=8).unsqueeze(2).to_broadcast([P, NT, NB, 8]),
+            )
+
+        def grp_of(key):
+            if ("g", key) not in live:
+                grp = grpp.tile([P, 4096], BF16, tag="grp", align_bytes=64)
+                live[("g", key)] = grp
+            return live[("g", key)]
+
+        def regroup_s(key, lo, hi):
+            dst4 = grp_of(key)[:].rearrange("p (k n t) -> p k n t", k=8, t=4)
+            for k in range(lo, hi):
+                nc.scalar.copy(
+                    out=dst4[:, k].rearrange("p (c i) t -> p c t i", i=4),
+                    in_=raws[key][:, k].rearrange("p t (c i) -> p c t i", i=4),
+                )
+
+        def regroup_v(key, nb):
+            dst4 = grp_of(key)[:].rearrange("p (k n t) -> p k n t", k=8, t=4)
+            nc.vector.tensor_copy(
+                out=dst4[:, 0:nb].rearrange("p k (c i) t -> p k c t i", i=4),
+                in_=raws[key][:, 0:nb].rearrange("p k t (c i) -> p k c t i", i=4),
+            )
+
+        def quantise_bulk(key):
+            grp = grp_of(key)
+            if key[0] == "w":
+                g = key[1]
+                nc.vector.quantize_mx(out=w2c[:, g, :].bitcast(FP8X4), scales=w2s[:, g, :], in_=grp[:])
+            else:
+                xc = xp.tile([P, 1024], U32, tag="xc", align_bytes=64)
+                xs = xp.tile([P, 1024], U8, tag="xs", align_bytes=64)
+                nc.vector.quantize_mx(out=xc[:].bitcast(FP8X4), scales=xs[:], in_=grp[:])
+                live[("c", key[1])] = (xc, xs)
+
+        def ff_transpose(t):
+            words = raws[("f", t)][:].bitcast(F32)
+            banks = []
+            for gp in range(2):
+                tp = psum.tile([P, 2, 2, P], F32, tag="tp")
+                for gq in range(2):
+                    for u in range(2):
+                        col = 256 * (2 * gp + gq)
+                        nc.tensor.transpose(tp[:, gq, u, :], words[:, col + u:col + 256:2], ident[:])
+                banks.append(tp)
+            live[("ftp", t)] = banks
+
+        def ff_out(t):
+            fg = work2.tile([P, 2048], BF16, tag="fg", align_bytes=64)
+            gw = fg[:].bitcast(F32).rearrange("p (g r u) -> p g r u", g=4, u=2)
+            for gp in range(2):
+                nc.scalar.copy(out=gw[:, 2 * gp:2 * gp + 2], in_=live[("ftp", t)][gp][:].rearrange("p g u r -> p g r u"))
+            live[("fg", t)] = fg
+
+        def ff_quantise(t):
+            nc.vector.quantize_mx(out=fc[:, t, :].bitcast(FP8X4), scales=fs[:, t, :], in_=live[("fg", t)][:])
+
+        def residual(t):
+            tgtb = work2.tile([P, D], F32, tag="tgtb")
+            nc.vector.tensor_tensor(out=tgtb[:], in0=raws[("t", t // 2)][:, t % 2, :], in1=b2bc[:], op=ALU.add)
+            live[("tgtb", t)] = tgtb
+
+        def stage1_mm(t):
+            banks = []
+            for h in range(2):
+                mm = psum.tile([P, 512], F32, tag="mm")
+                for g in range(4):
+                    nc.tensor.matmul_mx(
+                        out=mm[:],
+                        lhsT=fc[:, t, g * 128:(g + 1) * 128].bitcast(FP8X4),
+                        lhsT_scale=fs[:, t, g * 128:(g + 1) * 128],
+                        rhs=w2c[:, g, 512 * h:512 * h + 512].bitcast(FP8X4),
+                        rhs_scale=w2s[:, g, 512 * h:512 * h + 512],
+                        start=(g == 0),
+                        stop=(g == 3),
+                    )
+                banks.append(mm)
+            live[("mm", t)] = banks
+
+        def stage1_out(t):
+            u = work4.tile([P, D], F32, tag="u")
+            ssum = small.tile([P, 2], F32, tag="ssum")
+            tgtb = live[("tgtb", t)]
+            for h in range(2):
+                nc.vector.scalar_tensor_tensor(
+                    out=u[:, 512 * h:512 * h + 512].rearrange("p (t m) -> p m t", t=4),
+                    in0=live[("mm", t)][h][:].rearrange("p (m t) -> p m t", t=4),
+                    scalar=0.0,
+                    in1=tgtb[:, 512 * h:512 * h + 512].rearrange("p (m t) -> p m t", t=4),
+                    op0=ALU.add,
+                    op1=ALU.add,
+                    accum_out=ssum[:, h:h + 1],
+                )
+            negmean = small.tile([P, 1], F32, tag="negmean")
+            nc.vector.tensor_scalar(
+                out=negmean[:], in0=ssum[:, 0:1], scalar1=ssum[:, 1:2], scalar2=-1.0 / D,
+                op0=ALU.add, op1=ALU.mult,
+            )
+            live[("u", t)] = u
+            live[("negmean", t)] = negmean
+
+        def variance(t):
+            sq = work1.tile([P, D], BF16, tag="sq")
+            ssq = small.tile([P, 1], F32, tag="ssq")
+            nc.scalar.activation(
+                out=sq[:], in_=live[("u", t)][:], func=ACT.Square, bias=live[("negmean", t)][:], scale=1.0,
+                accum_out=ssq[:],
+            )
+            std = small.tile([P, 1], F32, tag="std")
+            nc.scalar.activation(out=std[:], in_=ssq[:], func=ACT.Sqrt, bias=eps[:], scale=1.0 / D)
+            live[("std", t)] = std
+
+        def norm_factors(t):
+            rstd = small.tile([P, 1], F32, tag="rstd")
+            nc.vector.reciprocal(out=rstd[:], in_=live[("std", t)][:])
+            nbias = small.tile([P, 1], F32, tag="nbias")
+            nc.scalar.activation(out=nbias[:], in_=live[("negmean", t)][:], func=ACT.Copy, scale=rstd[:, 0:1])
+            dg = work4.tile([P, P], F32, tag="dg")
+            nc.scalar.activation(out=dg[:], in_=perm[:], func=ACT.Copy, scale=rstd[:, 0:1])
+            live[("nbias", t)] = nbias
+            live[("dg", t)] = dg
+
+        def norm_flip(t):
+            banks = []
+            for bk in range(2):
+                zt = psum.tile([P, 4, P], F32, tag="zt")
+                for q in range(4):
+                    pl = 4 * bk + q
+                    nc.tensor.matmul(
+                        out=zt[:, q, :], lhsT=live[("u", t)][:, pl * 128:(pl + 1) * 128], rhs=live[("dg", t)][:],
+                        start=True, stop=False,
+                    )
+                    nc.tensor.matmul(
+                        out=zt[:, q, :], lhsT=live[("nbias", t)][:, 0:1].to_broadcast([P, P]), rhs=perm[:],
+                        is_transpose=True, start=False, stop=True,
+                    )
+                banks.append(zt)
+            live[("zt", t)] = banks
+
+        def gain_shift(t):
+            hTp = work2.tile([P, 8, P], BF16, tag="hTp")
+            for pl in range(8):
+                nc.scalar.activation(
+                    out=hTp[:, pl, :], in_=live[("zt", t)][pl // 4][:, pl % 4, :],
+                    func=ACT.Identity, bias=be3T[:, pl:pl + 1], scale=g3T[:, pl:pl + 1],
+                )
+            live[("hTp", t)] = hTp
+
+        def h_regroup(t):
+            hg = work2.tile([P, 1024], BF16, tag="hg", align_bytes=64)
+            nc.vector.tensor_copy(
+                out=hg[:].rearrange("p (c a i t) -> p c a t i", c=2, i=4, t=4),
+                in_=live[("hTp", t)][:].rearrange("p (c t) (a i) -> p c a t i", c=2, i=4),
+            )
+            live[("hg", t)] = hg
+
+        def h_quantise(t):
+            nc.vector.quantize_mx(out=hc[:, t, :].bitcast(FP8X4), scales=hs[:, t, :], in_=live[("hg", t)][:])
+
+        def stage2_mm(i):
+            banks = []
+            for hh in range(2):
+                s2 = psum.tile([P, 512], F32, tag="s2")
+                for kq in range(4):
+                    kk = 4 * hh + kq
+                    for c in range(2):
+                        xq = live[("c", 2 * i + c)]
+                        nc.tensor.matmul_mx(
+                            out=s2[:, kq * 128:(kq + 1) * 128],
+                            lhsT=xq[0][:, kk * 128:(kk + 1) * 128].bitcast(FP8X4),
+                            lhsT_scale=xq[1][:, kk * 128:(kk + 1) * 128],
+                            rhs=hc[:, i, c * 128:(c + 1) * 128].bitcast(FP8X4),
+                            rhs_scale=hs[:, i, c * 128:(c + 1) * 128],
+                            start=(c == 0),
+                            stop=(c == 1),
+                        )
+                banks.append(s2)
+            live[("s2", i)] = banks
+
+        def stage2_pick(i):
+            oT = work2.tile([P, P], F32, tag="oT")
+            for hh in range(2):
+                nc.scalar.copy(
+                    out=oT[:].rearrange("p (b k) -> p b k", k=8)[:, :, 4 * hh:4 * hh + 4],
+                    in_=live[("s2", i)][hh][:].rearrange("p (x y) -> p x y", y=16)[:, 4 * hh:4 * hh + 28:9, :].rearrange("p q b -> p b q"),
+                )
+            ot = psum.tile([P, P], F32, tag="tp")
+            nc.tensor.matmul(out=ot[:], lhsT=oT[:], rhs=ident[:], is_transpose=True, start=True, stop=False)
+            nc.tensor.matmul(out=ot[:], lhsT=bexp[:, i, :], rhs=ident[:], is_transpose=True, start=False, stop=True)
+            live[("ot", i)] = ot
+
+        def stage2_store(i):
+            nc.scalar.copy(out=o_all[:, i * 128:(i + 1) * 128], in_=live[("ot", i)][:])
+            nc.scalar.dma_start(out=outv[:, i * 128:(i + 1) * 128], in_=o_all[:, i * 128:(i + 1) * 128])
+
+        b2_spread()
+        for m in range(n_ticks):
+            key = plan[m] if m < len(plan) else None
+            prev = plan[m - 1] if 0 < m <= len(plan) else None
+            if tile_at(m, LAG["FT"]) >= 0:
+                ff_transpose(tile_at(m, LAG["FT"]))
+            for i in range(NT):
+                if o_tick[i] == m:
+                    stage2_mm(i)
+            if tile_at(m, LAG["E"]) >= 0:
+                stage1_out(tile_at(m, LAG["E"]))
+            if tile_at(m, LAG["SQ"]) >= 0:
+                variance(tile_at(m, LAG["SQ"]))
+            if key is not None:
+                regroup_s(key, V_BLOCKS, V_BLOCKS + S_FIRST)
+            for i in range(NT):
+                if o_tick[i] + LAG["OE"] == m:
+                    stage2_pick(i)
+            if tile_at(m, LAG["R"]) >= 0:
+                norm_factors(tile_at(m, LAG["R"]))
+                norm_flip(tile_at(m, LAG["R"]))
+            if key is not None:
+                regroup_v(key, V_BLOCKS)
+            if prev is not None:
+                quantise_bulk(prev)
+            if tile_at(m, LAG["MM"]) >= 0:
+                stage1_mm(tile_at(m, LAG["MM"]))
+            if tile_at(m, LAG["FE"]) >= 0:
+                ff_out(tile_at(m, LAG["FE"]))
+            if tile_at(m, LAG["T"]) >= 0:
+                residual(tile_at(m, LAG["T"]))
+            if m == CONST_TICK:
+                consts()
+            if tile_at(m, LAG["ZE"]) >= 0:
+                gain_shift(tile_at(m, LAG["ZE"]))
+            if tile_at(m, LAG["FQ"]) >= 0:
+                ff_quantise(tile_at(m, LAG["FQ"]))
+            if tile_at(m, LAG["HR"]) >= 0:
+                h_regroup(tile_at(m, LAG["HR"]))
+            if key is not None:
+                regroup_s(key, V_BLOCKS + S_FIRST, 8)
+            for i in range(NT):
+                if o_tick[i] + LAG["OC"] == m:
+                    stage2_store(i)
+            if tile_at(m, LAG["HQ"]) >= 0:
+                h_quantise(tile_at(m, LAG["HQ"]))

@@ -107,12 +107,23 @@ def tile_mldecoder_pb_kernel(tc, ff_hid, tgt, w2, b2, g3, be3, dup_pool, dup_bia
             idx = item[1][1]
             if kind == "w":
                 wraw = rawp.tile([P, 4, D], BF16, tag="raw")
-                nc.sync.dma_start(out=wraw[:].rearrange("p j n -> p (j n)"), in_=w2v[idx])
-                raws[item[1]] = wraw[:].rearrange("p t (k n) -> p k t n", k=8)
+                if idx == 0:
+                    halves = wraw[:].rearrange("p j n -> p (j n)").rearrange("p (h j n) -> p h j n", h=2, j=4)
+                    for h in range(2):
+                        nc.sync.dma_start(
+                            out=halves[:, h],
+                            in_=w2v[idx].rearrange("p (j n) -> p j n", j=4)[:, :, 512 * h:512 * h + 512],
+                        )
+                    raws[item[1]] = [halves[:, h].rearrange("p t (k n) -> p k t n", k=4) for h in range(2)]
+                else:
+                    nc.sync.dma_start(out=wraw[:].rearrange("p j n -> p (j n)"), in_=w2v[idx])
+                    whole = wraw[:].rearrange("p t (k n) -> p k t n", k=8)
+                    raws[item[1]] = [whole[:, 0:4], whole[:, 4:8]]
             elif kind == "x":
                 xraw = rawp.tile([P, 8, 512], BF16, tag="raw")
                 nc.sync.dma_start(out=xraw[:], in_=dv[idx // 2, idx % 2])
-                raws[item[1]] = xraw[:].rearrange("p k (t n) -> p k t n", t=4)
+                whole = xraw[:].rearrange("p k (t n) -> p k t n", t=4)
+                raws[item[1]] = [whole[:, 0:4], whole[:, 4:8]]
             elif kind == "f":
                 fraw = frawp.tile([P, FF], BF16, tag="fraw")
                 nc.sync.dma_start(out=fraw[:], in_=ffv[:, idx, :])
@@ -156,7 +167,7 @@ def tile_mldecoder_pb_kernel(tc, ff_hid, tgt, w2, b2, g3, be3, dup_pool, dup_bia
             for h in range(2):
                 bb = psum.tile([P, 512], F32, tag="mm")
                 nc.tensor.matmul(out=bb[:], lhsT=ones[:], rhs=brow[:, 512 * h:512 * h + 512], start=True, stop=True)
-                nc.scalar.copy(out=b2bc[:, 512 * h:512 * h + 512], in_=bb[:])
+                nc.vector.tensor_copy(out=b2bc[:, 512 * h:512 * h + 512], in_=bb[:])
 
         def consts():
             nc.vector.tensor_copy(out=g3T[:], in_=g3r[:].rearrange("p c t -> p (c t)"))
@@ -179,14 +190,14 @@ def tile_mldecoder_pb_kernel(tc, ff_hid, tgt, w2, b2, g3, be3, dup_pool, dup_bia
             for k in range(lo, hi):
                 nc.scalar.copy(
                     out=dst4[:, k].rearrange("p (c i) t -> p c t i", i=4),
-                    in_=raws[key][:, k].rearrange("p t (c i) -> p c t i", i=4),
+                    in_=raws[key][1][:, k - 4].rearrange("p t (c i) -> p c t i", i=4),
                 )
 
         def regroup_v(key, nb):
             dst4 = grp_of(key)[:].rearrange("p (k n t) -> p k n t", k=8, t=4)
             nc.vector.tensor_copy(
                 out=dst4[:, 0:nb].rearrange("p k (c i) t -> p k c t i", i=4),
-                in_=raws[key][:, 0:nb].rearrange("p k t (c i) -> p k c t i", i=4),
+                in_=raws[key][0][:, 0:nb].rearrange("p k t (c i) -> p k c t i", i=4),
             )
 
         def quantise_bulk(key):

@@ -24,13 +24,14 @@ FLOPS = 2 * NB * NK * FF * D + 2 * NB * NK * D * NG
 
 V_BLOCKS = 4
 S_FIRST = 1
-LAG = {"FT": 0, "FE": 2, "FQ": 3, "T": 3, "MM": 5, "E": 7, "SQ": 8, "R": 8, "ZE": 11, "HR": 11, "HQ": 12, "O2": 14, "OE": 3, "OC": 7}
+LAG = {"FT": 0, "FE": 2, "FQ": 3, "T": 3, "MM": 5, "E": 7, "SQ": 8, "R": 8, "ZE": 10, "HR": 10, "HQ": 11, "O2": 13, "OE": 2, "OC": 7}
 SPARSE_UNTIL = 18
 PRE_BULK = 4
 PRE_F = 2
 PRE_T = 4
 GAIN_LOAD_AFTER = 6
 CONST_TICK = 9
+LAST_X = 2 * NT - 2
 
 
 def bulk_plan():
@@ -121,7 +122,15 @@ def tile_mldecoder_pb_kernel(tc, ff_hid, tgt, w2, b2, g3, be3, dup_pool, dup_bia
                     raws[item[1]] = [whole[:, 0:4], whole[:, 4:8]]
             elif kind == "x":
                 xraw = rawp.tile([P, 8, 512], BF16, tag="raw")
-                nc.sync.dma_start(out=xraw[:], in_=dv[idx // 2, idx % 2])
+                if idx < LAST_X:
+                    nc.sync.dma_start(out=xraw[:], in_=dv[idx // 2, idx % 2])
+                else:
+                    for kp in range(2):
+                        for c in range(2):
+                            k0 = 4 * (idx - LAST_X) + 2 * kp
+                            nc.sync.dma_start(
+                                out=xraw[:, 4 * kp + 2 * c:4 * kp + 2 * c + 2, :], in_=dv[NT - 1, c][:, k0:k0 + 2, :],
+                            )
                 whole = xraw[:].rearrange("p k (t n) -> p k t n", t=4)
                 raws[item[1]] = [whole[:, 0:4], whole[:, 4:8]]
             elif kind == "f":
@@ -136,7 +145,7 @@ def tile_mldecoder_pb_kernel(tc, ff_hid, tgt, w2, b2, g3, be3, dup_pool, dup_bia
         eps = const.tile([P, 1], F32)
         nc.vector.memset(eps[:], EPS)
         warm = const.tile([P, 1], F32)
-        nc.scalar.activation(out=warm[:], in_=eps[:], func=ACT.Sqrt)
+        nc.scalar.activation(out=warm[:], in_=eps[:], func=ACT.Abs_reciprocal_sqrt)
         ident = const.tile([P, P], F32)
         make_identity(nc, ident[:])
         identb = const.tile([P, P], BF16)
@@ -208,7 +217,12 @@ def tile_mldecoder_pb_kernel(tc, ff_hid, tgt, w2, b2, g3, be3, dup_pool, dup_bia
             else:
                 xc = xp.tile([P, 1024], U32, tag="xc", align_bytes=64)
                 xs = xp.tile([P, 1024], U8, tag="xs", align_bytes=64)
-                nc.vector.quantize_mx(out=xc[:].bitcast(FP8X4), scales=xs[:], in_=grp[:])
+                for part in range(2 if key[1] == LAST_X + 1 else 1):
+                    n = 512 if key[1] == LAST_X + 1 else 1024
+                    nc.vector.quantize_mx(
+                        out=xc[:, n * part:n * part + n].bitcast(FP8X4), scales=xs[:, n * part:n * part + n],
+                        in_=grp[:, 4 * n * part:4 * n * part + 4 * n],
+                    )
                 live[("c", key[1])] = (xc, xs)
 
         def ff_transpose(t):
@@ -269,28 +283,28 @@ def tile_mldecoder_pb_kernel(tc, ff_hid, tgt, w2, b2, g3, be3, dup_pool, dup_bia
                     op1=ALU.add,
                     accum_out=ssum[:, h:h + 1],
                 )
-            negmean = small.tile([P, 1], F32, tag="negmean")
-            nc.vector.tensor_scalar(
-                out=negmean[:], in0=ssum[:, 0:1], scalar1=ssum[:, 1:2], scalar2=-1.0 / D,
-                op0=ALU.add, op1=ALU.mult,
-            )
             live[("u", t)] = u
-            live[("negmean", t)] = negmean
+            live[("ssum", t)] = ssum
 
         def variance(t):
+            negmean = small.tile([P, 1], F32, tag="negmean")
+            parts = small.tile([P, 2], F32, tag="parts")
+            nc.scalar.activation(
+                out=parts[:], in_=live[("ssum", t)][:], func=ACT.Copy, scale=-1.0 / D, accum_out=negmean[:],
+            )
+            live[("negmean", t)] = negmean
             sq = work1.tile([P, D], BF16, tag="sq")
             ssq = small.tile([P, 1], F32, tag="ssq")
             nc.scalar.activation(
                 out=sq[:], in_=live[("u", t)][:], func=ACT.Square, bias=live[("negmean", t)][:], scale=1.0,
                 accum_out=ssq[:],
             )
-            std = small.tile([P, 1], F32, tag="std")
-            nc.scalar.activation(out=std[:], in_=ssq[:], func=ACT.Sqrt, bias=eps[:], scale=1.0 / D)
-            live[("std", t)] = std
+            rstd = small.tile([P, 1], F32, tag="rstd")
+            nc.scalar.activation(out=rstd[:], in_=ssq[:], func=ACT.Abs_reciprocal_sqrt, bias=eps[:], scale=1.0 / D)
+            live[("rstd", t)] = rstd
 
         def norm_factors(t):
-            rstd = small.tile([P, 1], F32, tag="rstd")
-            nc.vector.reciprocal(out=rstd[:], in_=live[("std", t)][:])
+            rstd = live[("rstd", t)]
             nbias = small.tile([P, 1], F32, tag="nbias")
             nc.scalar.activation(out=nbias[:], in_=live[("negmean", t)][:], func=ACT.Copy, scale=rstd[:, 0:1])
             dg = work4.tile([P, P], F32, tag="dg")
@@ -335,32 +349,33 @@ def tile_mldecoder_pb_kernel(tc, ff_hid, tgt, w2, b2, g3, be3, dup_pool, dup_bia
         def h_quantise(t):
             nc.vector.quantize_mx(out=hc[:, t, :].bitcast(FP8X4), scales=hs[:, t, :], in_=live[("hg", t)][:])
 
-        def stage2_mm(i):
-            banks = []
-            for hh in range(2):
-                s2 = psum.tile([P, 512], F32, tag="s2")
-                for kq in range(4):
-                    kk = 4 * hh + kq
-                    for c in range(2):
+        def stage2_mm(i, hh):
+            s2 = psum.tile([P, 512], F32, tag="s2")
+            for kq in range(4):
+                for c in range(2):
+                    if i < NT - 1:
                         xq = live[("c", 2 * i + c)]
-                        nc.tensor.matmul_mx(
-                            out=s2[:, kq * 128:(kq + 1) * 128],
-                            lhsT=xq[0][:, kk * 128:(kk + 1) * 128].bitcast(FP8X4),
-                            lhsT_scale=xq[1][:, kk * 128:(kk + 1) * 128],
-                            rhs=hc[:, i, c * 128:(c + 1) * 128].bitcast(FP8X4),
-                            rhs_scale=hs[:, i, c * 128:(c + 1) * 128],
-                            start=(c == 0),
-                            stop=(c == 1),
-                        )
-                banks.append(s2)
-            live[("s2", i)] = banks
+                        blk = 4 * hh + kq
+                    else:
+                        xq = live[("c", LAST_X + hh)]
+                        blk = 4 * (kq // 2) + 2 * c + kq % 2
+                    nc.tensor.matmul_mx(
+                        out=s2[:, kq * 128:(kq + 1) * 128],
+                        lhsT=xq[0][:, blk * 128:(blk + 1) * 128].bitcast(FP8X4),
+                        lhsT_scale=xq[1][:, blk * 128:(blk + 1) * 128],
+                        rhs=hc[:, i, c * 128:(c + 1) * 128].bitcast(FP8X4),
+                        rhs_scale=hs[:, i, c * 128:(c + 1) * 128],
+                        start=(c == 0),
+                        stop=(c == 1),
+                    )
+            live[("s2", i, hh)] = s2
 
         def stage2_pick(i):
             oT = work2.tile([P, P], F32, tag="oT")
             for hh in range(2):
                 nc.scalar.copy(
                     out=oT[:].rearrange("p (b k) -> p b k", k=8)[:, :, 4 * hh:4 * hh + 4],
-                    in_=live[("s2", i)][hh][:].rearrange("p (x y) -> p x y", y=16)[:, 4 * hh:4 * hh + 28:9, :].rearrange("p q b -> p b q"),
+                    in_=live[("s2", i, hh)][:].rearrange("p (x y) -> p x y", y=16)[:, 4 * hh:4 * hh + 28:9, :].rearrange("p q b -> p b q"),
                 )
             ot = psum.tile([P, P], F32, tag="tp")
             nc.tensor.matmul(out=ot[:], lhsT=oT[:], rhs=ident[:], is_transpose=True, start=True, stop=False)
@@ -378,8 +393,9 @@ def tile_mldecoder_pb_kernel(tc, ff_hid, tgt, w2, b2, g3, be3, dup_pool, dup_bia
             if tile_at(m, LAG["FT"]) >= 0:
                 ff_transpose(tile_at(m, LAG["FT"]))
             for i in range(NT):
-                if o_tick[i] == m:
-                    stage2_mm(i)
+                for hh in range(2):
+                    if o_tick[i] - (1 if i == NT - 1 and hh == 0 else 0) == m:
+                        stage2_mm(i, hh)
             if tile_at(m, LAG["E"]) >= 0:
                 stage1_out(tile_at(m, LAG["E"]))
             if tile_at(m, LAG["SQ"]) >= 0:

from contextlib import ExitStack

import concourse.mybir as mybir
from concourse.masks import make_identity

F32 = mybir.dt.float32
BF16 = mybir.dt.bfloat16
U32 = mybir.dt.uint32
U8 = mybir.dt.uint8
I32 = mybir.dt.int32
FP8X4 = mybir.dt.float8_e4m3fn_x4
ALU = mybir.AluOpType
ACT = mybir.ActivationFunctionType

P = 128
NB = 16
NK = 64
NG = 128
D = 1024
FF = 2048
NT = 8
EPS = 1e-5
FLOPS = 2 * NB * NK * FF * D + 2 * NB * NK * D * NG

V_BLOCKS = 4
S_FIRST = 1
LAG = {"FT": 0, "FE": 2, "FQ": 3, "T": 3, "MM": 5, "E": 7, "SQ": 8, "R": 8, "ZE": 10, "HR": 10, "HQ": 11, "O2": 13, "OE": 2, "OC": 7}
SPARSE_UNTIL = 18
PRE_BULK = 4
PRE_F = 2
PRE_T = 4
GAIN_LOAD_AFTER = 6
CONST_TICK = 9
LAST_X = 2 * NT - 2


def bulk_plan():
    plan = [("w", g) for g in range(4)]
    s = 0
    while s < 16:
        m = len(plan)
        if m < SPARSE_UNTIL and m % 2 == 0:
            plan.append(None)
        else:
            plan.append(("x", s))
            s += 1
    return plan


def tile_at(m, lag):
    t = m - lag
    if t >= 0 and t % 2 == 0 and t // 2 < NT:
        return t // 2
    return -1


def tile_mldecoder_pb_kernel(tc, ff_hid, tgt, w2, b2, g3, be3, dup_pool, dup_bias, out):
    nc = tc.nc
    ffv = ff_hid.rearrange("b (kk i) f -> (b kk) i f", i=8)
    tgv = tgt.rearrange("b (kk i) d -> (b kk) i d", i=8)
    w2v = w2.rearrange("(g p j) n -> g p (j n)", g=4, j=4)
    dv = dup_pool.rearrange("(kk i) (c p j) g -> i c p kk (j g)", i=8, c=2, j=4)
    outv = out.rearrange("b (kk x) -> (b kk) x", kk=8)
    plan = bulk_plan()
    q_tick = {}
    for m in range(len(plan)):
        if plan[m] is not None:
            q_tick[plan[m]] = m + 1
    o_tick = [max(2 * i + LAG["O2"], q_tick[("x", 2 * i + 1)] + 1) for i in range(NT)]
    n_ticks = max(o_tick) + LAG["OC"] + 1

    with ExitStack() as ctx:
        const = ctx.enter_context(tc.tile_pool(name="const", bufs=1))
        keep = ctx.enter_context(tc.tile_pool(name="keep", bufs=1))
        rawp = ctx.enter_context(tc.tile_pool(name="rawp", bufs=6))
        frawp = ctx.enter_context(tc.tile_pool(name="frawp", bufs=3))
        grpp = ctx.enter_context(tc.tile_pool(name="grpp", bufs=3))
        xp = ctx.enter_context(tc.tile_pool(name="xp", bufs=5))
        work1 = ctx.enter_context(tc.tile_pool(name="work1", bufs=1))
        work2 = ctx.enter_context(tc.tile_pool(name="work2", bufs=2))
        work4 = ctx.enter_context(tc.tile_pool(name="work4", bufs=4))
        small = ctx.enter_context(tc.tile_pool(name="small", bufs=4))
        psum = ctx.enter_context(tc.psum_pool(name="psum", bufs=2))

        brow = grpp.tile([P, 4096], BF16, tag="grp", align_bytes=64)
        nc.vector.memset(brow[:, 0:D].bitcast(I32), 0)
        nc.sync.dma_start(out=brow[0:1, 0:D], in_=b2.rearrange("(o d) -> o d", o=1))
        g3r = const.tile([P, 2, 4], BF16)
        be3r = const.tile([P, 2, 4], BF16)
        braw = const.tile([P, P], BF16)
        nc.vector.memset(braw[:].bitcast(I32), 0)
        nc.sync.dma_start(out=braw[0:NK, :], in_=dup_bias.rearrange("(k g) -> k g", g=NG))

        wanted = []
        for m in range(len(plan)):
            if plan[m] is not None:
                wanted.append((m - PRE_BULK, plan[m]))
        for t in range(NT):
            wanted.append((2 * t + LAG["FT"] - PRE_F, ("f", t)))
            if t % 2 == 0:
                wanted.append((2 * t + LAG["T"] - PRE_T, ("t", t // 2)))
        raws = {}
        for item in sorted(wanted, key=lambda pair: pair[0]):
            if len(raws) == GAIN_LOAD_AFTER:
                nc.sync.dma_start(out=g3r[:], in_=g3.rearrange("(c p t) -> p c t", c=2, t=4))
                nc.sync.dma_start(out=be3r[:], in_=be3.rearrange("(c p t) -> p c t", c=2, t=4))
            kind = item[1][0]
            idx = item[1][1]
            if kind == "w":
                wraw = rawp.tile([P, 4, D], BF16, tag="raw")
                if idx == 0:
                    halves = wraw[:].rearrange("p j n -> p (j n)").rearrange("p (h j n) -> p h j n", h=2, j=4)
                    for h in range(2):
                        nc.sync.dma_start(
                            out=halves[:, h],
                            in_=w2v[idx].rearrange("p (j n) -> p j n", j=4)[:, :, 512 * h:512 * h + 512],
                        )
                    raws[item[1]] = [halves[:, h].rearrange("p t (k n) -> p k t n", k=4) for h in range(2)]
                else:
                    nc.sync.dma_start(out=wraw[:].rearrange("p j n -> p (j n)"), in_=w2v[idx])
                    whole = wraw[:].rearrange("p t (k n) -> p k t n", k=8)
                    raws[item[1]] = [whole[:, 0:4], whole[:, 4:8]]
            elif kind == "x":
                xraw = rawp.tile([P, 8, 512], BF16, tag="raw")
                if idx < LAST_X:
                    nc.sync.dma_start(out=xraw[:], in_=dv[idx // 2, idx % 2])
                else:
                    for kp in range(2):
                        for c in range(2):
                            k0 = 4 * (idx - LAST_X) + 2 * kp
                            nc.sync.dma_start(
                                out=xraw[:, 4 * kp + 2 * c:4 * kp + 2 * c + 2, :], in_=dv[NT - 1, c][:, k0:k0 + 2, :],
                            )
                whole = xraw[:].rearrange("p k (t n) -> p k t n", t=4)
                raws[item[1]] = [whole[:, 0:4], whole[:, 4:8]]
            elif kind == "f":
                fraw = frawp.tile([P, FF], BF16, tag="fraw")
                nc.sync.dma_start(out=fraw[:], in_=ffv[:, idx, :])
                raws[item[1]] = fraw
            else:
                traw = work2.tile([P, 2, D], BF16, tag="traw")
                nc.sync.dma_start(out=traw[:], in_=tgv[:, 2 * idx:2 * idx + 2, :])
                raws[item[1]] = traw

        eps = const.tile([P, 1], F32)
        nc.vector.memset(eps[:], EPS)
        warm = const.tile([P, 1], F32)
        nc.scalar.activation(out=warm[:], in_=eps[:], func=ACT.Abs_reciprocal_sqrt)
        ident = const.tile([P, P], F32)
        make_identity(nc, ident[:])
        identb = const.tile([P, P], BF16)
        make_identity(nc, identb[:])
        perm = const.tile([P, P], F32)
        nc.vector.tensor_copy(
            out=perm[:].rearrange("p (k b) -> p k b", k=8),
            in_=ident[:].rearrange("p (b k) -> p k b", k=8),
        )
        ones = const.tile([P, P], BF16)
        nc.vector.memset(ones[:], 1.0)
        b2bc = const.tile([P, D], BF16)
        g3T = const.tile([P, 8], F32)
        be3T = const.tile([P, 8], F32)
        bexp = const.tile([P, NT, P], F32)
        o_all = const.tile([P, D], F32)

        w2c = keep.tile([P, 4, D], U32, align_bytes=64)
        w2s = keep.tile([P, 4, D], U8, align_bytes=64)
        fc = keep.tile([P, NT, 512], U32, align_bytes=64)
        fs = keep.tile([P, NT, 512], U8, align_bytes=64)
        hc = keep.tile([P, NT, 256], U32, align_bytes=64)
        hs = keep.tile([P, NT, 256], U8, align_bytes=64)

        live = {}

        def b2_spread():
            for h in range(2):
                bb = psum.tile([P, 512], F32, tag="mm")
                nc.tensor.matmul(out=bb[:], lhsT=ones[:], rhs=brow[:, 512 * h:512 * h + 512], start=True, stop=True)
                nc.vector.tensor_copy(out=b2bc[:, 512 * h:512 * h + 512], in_=bb[:])

        def consts():
            nc.vector.tensor_copy(out=g3T[:], in_=g3r[:].rearrange("p c t -> p (c t)"))
            nc.vector.tensor_copy(out=be3T[:], in_=be3r[:].rearrange("p c t -> p (c t)"))
            bps = psum.tile([P, P], BF16, tag="s2")
            nc.tensor.transpose(bps[:], braw[:], identb[:])
            nc.scalar.copy(
                out=bexp[:].rearrange("p i (b k) -> p i b k", k=8),
                in_=bps[:, 0:NK].rearrange("p (k i) -> p i k", i=8).unsqueeze(2).to_broadcast([P, NT, NB, 8]),
            )

        def grp_of(key):
            if ("g", key) not in live:
                grp = grpp.tile([P, 4096], BF16, tag="grp", align_bytes=64)
                live[("g", key)] = grp
            return live[("g", key)]

        def regroup_s(key, lo, hi):
            dst4 = grp_of(key)[:].rearrange("p (k n t) -> p k n t", k=8, t=4)
            for k in range(lo, hi):
                nc.scalar.copy(
                    out=dst4[:, k].rearrange("p (c i) t -> p c t i", i=4),
                    in_=raws[key][1][:, k - 4].rearrange("p t (c i) -> p c t i", i=4),
                )

        def regroup_v(key, nb):
            dst4 = grp_of(key)[:].rearrange("p (k n t) -> p k n t", k=8, t=4)
            nc.vector.tensor_copy(
                out=dst4[:, 0:nb].rearrange("p k (c i) t -> p k c t i", i=4),
                in_=raws[key][0][:, 0:nb].rearrange("p k t (c i) -> p k c t i", i=4),
            )

        def quantise_bulk(key):
            grp = grp_of(key)
            if key[0] == "w":
                g = key[1]
                nc.vector.quantize_mx(out=w2c[:, g, :].bitcast(FP8X4), scales=w2s[:, g, :], in_=grp[:])
            else:
                xc = xp.tile([P, 1024], U32, tag="xc", align_bytes=64)
                xs = xp.tile([P, 1024], U8, tag="xs", align_bytes=64)
                for part in range(2 if key[1] == LAST_X + 1 else 1):
                    n = 512 if key[1] == LAST_X + 1 else 1024
                    nc.vector.quantize_mx(
                        out=xc[:, n * part:n * part + n].bitcast(FP8X4), scales=xs[:, n * part:n * part + n],
                        in_=grp[:, 4 * n * part:4 * n * part + 4 * n],
                    )
                live[("c", key[1])] = (xc, xs)

        def ff_transpose(t):
            words = raws[("f", t)][:].bitcast(F32)
            banks = []
            for gp in range(2):
                tp = psum.tile([P, 2, 2, P], F32, tag="tp")
                for gq in range(2):
                    for u in range(2):
                        col = 256 * (2 * gp + gq)
                        nc.tensor.transpose(tp[:, gq, u, :], words[:, col + u:col + 256:2], ident[:])
                banks.append(tp)
            live[("ftp", t)] = banks

        def ff_out(t):
            fg = work2.tile([P, 2048], BF16, tag="fg", align_bytes=64)
            gw = fg[:].bitcast(F32).rearrange("p (g r u) -> p g r u", g=4, u=2)
            for gp in range(2):
                nc.scalar.copy(out=gw[:, 2 * gp:2 * gp + 2], in_=live[("ftp", t)][gp][:].rearrange("p g u r -> p g r u"))
            live[("fg", t)] = fg

        def ff_quantise(t):
            nc.vector.quantize_mx(out=fc[:, t, :].bitcast(FP8X4), scales=fs[:, t, :], in_=live[("fg", t)][:])

        def residual(t):
            tgtb = work2.tile([P, D], F32, tag="tgtb")
            nc.vector.tensor_tensor(out=tgtb[:], in0=raws[("t", t // 2)][:, t % 2, :], in1=b2bc[:], op=ALU.add)
            live[("tgtb", t)] = tgtb

        def stage1_mm(t):
            banks = []
            for h in range(2):
                mm = psum.tile([P, 512], F32, tag="mm")
                for g in range(4):
                    nc.tensor.matmul_mx(
                        out=mm[:],
                        lhsT=fc[:, t, g * 128:(g + 1) * 128].bitcast(FP8X4),
                        lhsT_scale=fs[:, t, g * 128:(g + 1) * 128],
                        rhs=w2c[:, g, 512 * h:512 * h + 512].bitcast(FP8X4),
                        rhs_scale=w2s[:, g, 512 * h:512 * h + 512],
                        start=(g == 0),
                        stop=(g == 3),
                    )
                banks.append(mm)
            live[("mm", t)] = banks

        def stage1_out(t):
            u = work4.tile([P, D], F32, tag="u")
            ssum = small.tile([P, 2], F32, tag="ssum")
            tgtb = live[("tgtb", t)]
            for h in range(2):
                nc.vector.scalar_tensor_tensor(
                    out=u[:, 512 * h:512 * h + 512].rearrange("p (t m) -> p m t", t=4),
                    in0=live[("mm", t)][h][:].rearrange("p (m t) -> p m t", t=4),
                    scalar=0.0,
                    in1=tgtb[:, 512 * h:512 * h + 512].rearrange("p (m t) -> p m t", t=4),
                    op0=ALU.add,
                    op1=ALU.add,
                    accum_out=ssum[:, h:h + 1],
                )
            live[("u", t)] = u
            live[("ssum", t)] = ssum

        def variance(t):
            negmean = small.tile([P, 1], F32, tag="negmean")
            parts = small.tile([P, 2], F32, tag="parts")
            nc.scalar.activation(
                out=parts[:], in_=live[("ssum", t)][:], func=ACT.Copy, scale=-1.0 / D, accum_out=negmean[:],
            )
            live[("negmean", t)] = negmean
            sq = work1.tile([P, D], BF16, tag="sq")
            ssq = small.tile([P, 1], F32, tag="ssq")
            nc.scalar.activation(
                out=sq[:], in_=live[("u", t)][:], func=ACT.Square, bias=live[("negmean", t)][:], scale=1.0,
                accum_out=ssq[:],
            )
            rstd = small.tile([P, 1], F32, tag="rstd")
            nc.scalar.activation(out=rstd[:], in_=ssq[:], func=ACT.Abs_reciprocal_sqrt, bias=eps[:], scale=1.0 / D)
            live[("rstd", t)] = rstd

        def norm_factors(t):
            rstd = live[("rstd", t)]
            nbias = small.tile([P, 1], F32, tag="nbias")
            nc.scalar.activation(out=nbias[:], in_=live[("negmean", t)][:], func=ACT.Copy, scale=rstd[:, 0:1])
            dg = work4.tile([P, P], F32, tag="dg")
            nc.scalar.activation(out=dg[:], in_=perm[:], func=ACT.Copy, scale=rstd[:, 0:1])
            live[("nbias", t)] = nbias
            live[("dg", t)] = dg

        def norm_flip(t):
            banks = []
            for bk in range(2):
                zt = psum.tile([P, 4, P], F32, tag="zt")
                for q in range(4):
                    pl = 4 * bk + q
                    nc.tensor.matmul(
                        out=zt[:, q, :], lhsT=live[("u", t)][:, pl * 128:(pl + 1) * 128], rhs=live[("dg", t)][:],
                        start=True, stop=False,
                    )
                    nc.tensor.matmul(
                        out=zt[:, q, :], lhsT=live[("nbias", t)][:, 0:1].to_broadcast([P, P]), rhs=perm[:],
                        is_transpose=True, start=False, stop=True,
                    )
                banks.append(zt)
            live[("zt", t)] = banks

        def gain_shift(t):
            hTp = work2.tile([P, 8, P], BF16, tag="hTp")
            for pl in range(8):
                nc.scalar.activation(
                    out=hTp[:, pl, :], in_=live[("zt", t)][pl // 4][:, pl % 4, :],
                    func=ACT.Identity, bias=be3T[:, pl:pl + 1], scale=g3T[:, pl:pl + 1],
                )
            live[("hTp", t)] = hTp

        def h_regroup(t):
            hg = work2.tile([P, 1024], BF16, tag="hg", align_bytes=64)
            nc.vector.tensor_copy(
                out=hg[:].rearrange("p (c a i t) -> p c a t i", c=2, i=4, t=4),
                in_=live[("hTp", t)][:].rearrange("p (c t) (a i) -> p c a t i", c=2, i=4),
            )
            live[("hg", t)] = hg

        def h_quantise(t):
            nc.vector.quantize_mx(out=hc[:, t, :].bitcast(FP8X4), scales=hs[:, t, :], in_=live[("hg", t)][:])

        def stage2_mm(i, hh):
            s2 = psum.tile([P, 512], F32, tag="s2")
            for kq in range(4):
                for c in range(2):
                    if i < NT - 1:
                        xq = live[("c", 2 * i + c)]
                        blk = 4 * hh + kq
                    else:
                        xq = live[("c", LAST_X + hh)]
                        blk = 4 * (kq // 2) + 2 * c + kq % 2
                    nc.tensor.matmul_mx(
                        out=s2[:, kq * 128:(kq + 1) * 128],
                        lhsT=xq[0][:, blk * 128:(blk + 1) * 128].bitcast(FP8X4),
                        lhsT_scale=xq[1][:, blk * 128:(blk + 1) * 128],
                        rhs=hc[:, i, c * 128:(c + 1) * 128].bitcast(FP8X4),
                        rhs_scale=hs[:, i, c * 128:(c + 1) * 128],
                        start=(c == 0),
                        stop=(c == 1),
                    )
            live[("s2", i, hh)] = s2

        def stage2_pick(i):
            oT = work2.tile([P, P], F32, tag="oT")
            for hh in range(2):
                nc.scalar.copy(
                    out=oT[:].rearrange("p (b k) -> p b k", k=8)[:, :, 4 * hh:4 * hh + 4],
                    in_=live[("s2", i, hh)][:].rearrange("p (x y) -> p x y", y=16)[:, 4 * hh:4 * hh + 28:9, :].rearrange("p q b -> p b q"),
                )
            ot = psum.tile([P, P], F32, tag="tp")
            nc.tensor.matmul(out=ot[:], lhsT=oT[:], rhs=ident[:], is_transpose=True, start=True, stop=False)
            nc.tensor.matmul(out=ot[:], lhsT=bexp[:, i, :], rhs=ident[:], is_transpose=True, start=False, stop=True)
            live[("ot", i)] = ot

        def stage2_store(i):
            nc.scalar.copy(out=o_all[:, i * 128:(i + 1) * 128], in_=live[("ot", i)][:])
            nc.scalar.dma_start(out=outv[:, i * 128:(i + 1) * 128], in_=o_all[:, i * 128:(i + 1) * 128])

        b2_spread()
        for m in range(n_ticks):
            key = plan[m] if m < len(plan) else None
            prev = plan[m - 1] if 0 < m <= len(plan) else None
            if tile_at(m, LAG["FT"]) >= 0:
                ff_transpose(tile_at(m, LAG["FT"]))
            for i in range(NT):
                for hh in range(2):
                    if o_tick[i] - (1 if i == NT - 1 and hh == 0 else 0) == m:
                        stage2_mm(i, hh)
            if tile_at(m, LAG["E"]) >= 0:
                stage1_out(tile_at(m, LAG["E"]))
            if tile_at(m, LAG["SQ"]) >= 0:
                variance(tile_at(m, LAG["SQ"]))
            if key is not None:
                regroup_s(key, V_BLOCKS, V_BLOCKS + S_FIRST)
            for i in range(NT):
                if o_tick[i] + LAG["OE"] == m:
                    stage2_pick(i)
            if tile_at(m, LAG["R"]) >= 0:
                norm_factors(tile_at(m, LAG["R"]))
                norm_flip(tile_at(m, LAG["R"]))
            if key is not None:
                regroup_v(key, V_BLOCKS)
            if prev is not None:
                quantise_bulk(prev)
            if tile_at(m, LAG["MM"]) >= 0:
                stage1_mm(tile_at(m, LAG["MM"]))
            if tile_at(m, LAG["FE"]) >= 0:
                ff_out(tile_at(m, LAG["FE"]))
            if tile_at(m, LAG["T"]) >= 0:
                residual(tile_at(m, LAG["T"]))
            if m == CONST_TICK:
                consts()
            if tile_at(m, LAG["ZE"]) >= 0:
                gain_shift(tile_at(m, LAG["ZE"]))
            if tile_at(m, LAG["FQ"]) >= 0:
                ff_quantise(tile_at(m, LAG["FQ"]))
            if tile_at(m, LAG["HR"]) >= 0:
                h_regroup(tile_at(m, LAG["HR"]))
            if key is not None:
                regroup_s(key, V_BLOCKS + S_FIRST, 8)
            for i in range(NT):
                if o_tick[i] + LAG["OC"] == m:
                    stage2_store(i)
            if tile_at(m, LAG["HQ"]) >= 0:
                h_quantise(tile_at(m, LAG["HQ"]))
